import numpy as np
import ml_dtypes

BF16 = ml_dtypes.bfloat16


def bf(x):
    return np.asarray(x, np.float32).astype(BF16)


def f32(x):
    return np.asarray(x, np.float32)


def f64(x):
    return np.asarray(x).astype(np.float64)


def striped(idx):
    return np.tile(idx.reshape(-1, 16).T, (8, 1))


V, D, NKV, HD, HALF, M, N = 1024, 128, 8, 64, 32, 512, 512
EPS = 1e-5


def setup_inputs():
    ang = np.random.uniform(0.0, 2.0 * np.pi, (HALF, 1))
    return {"table": bf(0.02 * np.random.standard_normal((V, D))), "gain": f32(1.0 + 0.1 * np.random.standard_normal((D, 1))), "wk": bf(np.random.standard_normal((D, M)) / np.sqrt(D)), "cosv": f32(np.cos(ang)), "sinv": f32(np.sin(ang)), "offs": striped(np.random.permutation(np.tile(np.arange(V), 2))[:N])}


def reference(table, gain, wk, cosv, sinv, offs):
    idx = offs[:16].T.reshape(-1)
    t = f64(table)
    xn = t / np.sqrt(np.mean(t * t, axis=1, keepdims=True) + EPS) * f64(gain)[:, 0]
    k = (f64(wk).T @ xn[idx].T).reshape(NKV, HD, N)
    kr, ki = k[:, 0::2], k[:, 1::2]
    c, s = f64(cosv)[None], f64(sinv)[None]
    return np.concatenate([kr * c - ki * s, kr * s + ki * c], axis=1).reshape(M, N)

@@ -1,0 +1,105 @@
+import concourse.mybir as mybir
+from concourse.masks import make_identity
+
+P = 128
+V, D, M, N = 1024, 128, 512, 512
+HALF = 32
+EPS = 1e-5
+FLOPS = 2 * D * M * N
+
+BF16, F32, U16 = mybir.dt.bfloat16, mybir.dt.float32, mybir.dt.uint16
+MULT, ADD, SUBTRACT = mybir.AluOpType.mult, mybir.AluOpType.add, mybir.AluOpType.subtract
+ACT = mybir.ActivationFunctionType
+
+BLOCKS = V // P
+PAIRS = M // 2
+GROUPS = PAIRS // P
+HEADS_IN_GROUP = P // HALF
+
+
+def tile_llamamodel_kernel(tc, table, gain, wk, cosv, sinv, offs, out):
+    nc = tc.nc
+    with (
+        tc.tile_pool(name="held", bufs=1) as held,
+        tc.tile_pool(name="work", bufs=2) as work,
+        tc.psum_pool(name="flip", bufs=4) as flip,
+        tc.psum_pool(name="keys", bufs=2) as keys,
+    ):
+        offsets = held.tile([P, N // 16], U16, name="offsets")
+        nc.sync.dma_start(offsets[:], offs)
+
+        rows = held.tile([P, BLOCKS, D], BF16, name="rows")
+        table_blocks = table.rearrange("(t p) d -> p t d", p=P)
+        nc.sync.dma_start(rows[:, 0 : BLOCKS // 2, :], table_blocks[:, 0 : BLOCKS // 2, :])
+        nc.scalar.dma_start(rows[:, BLOCKS // 2 : BLOCKS, :], table_blocks[:, BLOCKS // 2 : BLOCKS, :])
+
+        gain_all = held.tile([P, D], F32, name="gain_all")
+        nc.scalar.dma_start(gain_all[:], gain.rearrange("d o -> (d o)").partition_broadcast(P))
+
+        wk_sb = held.tile([D, M], BF16, name="wk_sb")
+        nc.gpsimd.dma_start(wk_sb[:], wk)
+
+        cos_col = held.tile([P, 1], F32, name="cos_col")
+        sin_col = held.tile([P, 1], F32, name="sin_col")
+        for q in range(HEADS_IN_GROUP):
+            nc.gpsimd.dma_start(cos_col[q * HALF : (q + 1) * HALF, :], cosv)
+            nc.gpsimd.dma_start(sin_col[q * HALF : (q + 1) * HALF, :], sinv)
+
+        identity = held.tile([P, P], BF16, name="identity")
+        make_identity(nc, identity[:])
+
+        wk_split = held.tile([D, 2, PAIRS], BF16, name="wk_split")
+        nc.gpsimd.tensor_copy(wk_split[:], wk_sb[:].rearrange("d (q two) -> d two q", two=2))
+
+        PER_ENGINE = BLOCKS // 2
+        sumsq = held.tile([P, 2, 8], F32, name="sumsq")
+        for k in range(PER_ENGINE):
+            sq_act = work.tile([P, D], F32, name="sq_act")
+            nc.scalar.activation(sq_act[:], rows[:, k, :], ACT.Square, accum_out=sumsq[:, 0, k : k + 1])
+            sq_dve = work.tile([P, D], F32, name="sq_dve")
+            nc.vector.scalar_tensor_tensor(
+                sq_dve[:], rows[:, PER_ENGINE + k, :], 1.0, rows[:, PER_ENGINE + k, :], MULT, MULT,
+                accum_out=sumsq[:, 1, k : k + 1],
+            )
+        rms = held.tile([P, 2, PER_ENGINE], F32, name="rms")
+        nc.scalar.activation(rms[:], sumsq[:, :, 0:PER_ENGINE], ACT.Sqrt, bias=EPS, scale=1.0 / D)
+        rstd = held.tile([P, BLOCKS], F32, name="rstd")
+        nc.vector.reciprocal(rstd[:], rms[:].rearrange("p e k -> p (e k)"))
+
+        xn = held.tile([P, BLOCKS, D], BF16, name="xn")
+        for t in range(BLOCKS):
+            nc.vector.scalar_tensor_tensor(
+                xn[:, t, :], rows[:, t, :], rstd[:, t : t + 1], gain_all[:], MULT, MULT
+            )
+
+        window = held.tile([D, V], BF16, name="window")
+        for g in range(BLOCKS // 2):
+            flipped = flip.tile([D, 2 * P], BF16, name="flipped")
+            for t in (2 * g, 2 * g + 1):
+                nc.tensor.transpose(flipped[:, (t % 2) * P : (t % 2 + 1) * P], xn[:, t, :], identity[:])
+            if g % 2 == 0:
+                nc.vector.tensor_copy(window[:, g * 2 * P : (g + 1) * 2 * P], flipped[:])
+            else:
+                nc.scalar.copy(window[:, g * 2 * P : (g + 1) * 2 * P], flipped[:])
+
+        out_rows = out.rearrange("(b q half i) j -> b half q i j", b=GROUPS, q=HEADS_IN_GROUP, half=2, i=HALF)
+        for b in range(GROUPS):
+            k_odd = keys.tile([P, N], F32, name="k_odd")
+            nc.tensor.matmul(
+                k_odd[:], wk_split[:, 1, b * P : (b + 1) * P], window[:].indirect(offsets[:]), start=True, stop=True
+            )
+            k_even = keys.tile([P, N], F32, name="k_even")
+            nc.tensor.matmul(
+                k_even[:], wk_split[:, 0, b * P : (b + 1) * P], window[:].indirect(offsets[:]), start=True, stop=True
+            )
+            odd_sin = work.tile([P, N], F32, name="odd_sin")
+            nc.scalar.activation(odd_sin[:], k_odd[:], ACT.Copy, scale=sin_col[:, 0:1])
+            odd_cos = work.tile([P, N], F32, name="odd_cos")
+            nc.scalar.activation(odd_cos[:], k_odd[:], ACT.Copy, scale=cos_col[:, 0:1])
+            first = work.tile([P, N], F32, name="first")
+            nc.vector.scalar_tensor_tensor(first[:], k_even[:], cos_col[:, 0:1], odd_sin[:], MULT, SUBTRACT)
+            second = work.tile([P, N], F32, name="second")
+            nc.vector.scalar_tensor_tensor(second[:], k_even[:], sin_col[:, 0:1], odd_cos[:], MULT, ADD)
+            for half, rotated in enumerate((first, second)):
+                for q in range(HEADS_IN_GROUP):
+                    nc.sync.dma_start(out_rows[b, half, q], rotated[q * HALF : (q + 1) * HALF, :])

@@ -25,6 +25,9 @@ def tile_llamamodel_kernel(tc, table, gain, wk, cosv, sinv, offs, out):
         tc.psum_pool(name="flip", bufs=4) as flip,
         tc.psum_pool(name="keys", bufs=2) as keys,
     ):
+        identity = held.tile([P, P], BF16, name="identity")
+        make_identity(nc, identity[:])
+
         offsets = held.tile([P, N // 16], U16, name="offsets")
         nc.sync.dma_start(offsets[:], offs)
 
@@ -37,16 +40,13 @@ def tile_llamamodel_kernel(tc, table, gain, wk, cosv, sinv, offs, out):
         nc.scalar.dma_start(gain_all[:], gain.rearrange("d o -> (d o)").partition_broadcast(P))
 
         wk_sb = held.tile([D, M], BF16, name="wk_sb")
-        nc.gpsimd.dma_start(wk_sb[:], wk)
+        nc.sync.dma_start(wk_sb[:], wk)
 
         cos_col = held.tile([P, 1], F32, name="cos_col")
         sin_col = held.tile([P, 1], F32, name="sin_col")
         for q in range(HEADS_IN_GROUP):
-            nc.gpsimd.dma_start(cos_col[q * HALF : (q + 1) * HALF, :], cosv)
-            nc.gpsimd.dma_start(sin_col[q * HALF : (q + 1) * HALF, :], sinv)
-
-        identity = held.tile([P, P], BF16, name="identity")
-        make_identity(nc, identity[:])
+            nc.sync.dma_start(cos_col[q * HALF : (q + 1) * HALF, :], cosv)
+            nc.sync.dma_start(sin_col[q * HALF : (q + 1) * HALF, :], sinv)
 
         wk_split = held.tile([D, 2, PAIRS], BF16, name="wk_split")
         nc.gpsimd.tensor_copy(wk_split[:], wk_sb[:].rearrange("d (q two) -> d two q", two=2))

@@ -12,6 +12,7 @@ MULT, ADD, SUBTRACT = mybir.AluOpType.mult, mybir.AluOpType.add, mybir.AluOpType
 ACT = mybir.ActivationFunctionType
 
 BLOCKS = V // P
+PER_ENGINE = BLOCKS // 2
 PAIRS = M // 2
 GROUPS = PAIRS // P
 HEADS_IN_GROUP = P // HALF
@@ -25,19 +26,19 @@ def tile_llamamodel_kernel(tc, table, gain, wk, cosv, sinv, offs, out):
         tc.psum_pool(name="flip", bufs=4) as flip,
         tc.psum_pool(name="keys", bufs=2) as keys,
     ):
-        identity = held.tile([P, P], BF16, name="identity")
+        identity = held.tile([P, P], F32, name="identity")
         make_identity(nc, identity[:])
+
+        rows = held.tile([P, BLOCKS, D], BF16, name="rows")
+        table_blocks = table.rearrange("(t p) d -> p t d", p=P)
+        nc.sync.dma_start(rows[:, 0:PER_ENGINE, :], table_blocks[:, 0:PER_ENGINE, :])
+        nc.scalar.dma_start(rows[:, PER_ENGINE:BLOCKS, :], table_blocks[:, PER_ENGINE:BLOCKS, :])
 
         offsets = held.tile([P, N // 16], U16, name="offsets")
         nc.sync.dma_start(offsets[:], offs)
 
-        rows = held.tile([P, BLOCKS, D], BF16, name="rows")
-        table_blocks = table.rearrange("(t p) d -> p t d", p=P)
-        nc.sync.dma_start(rows[:, 0 : BLOCKS // 2, :], table_blocks[:, 0 : BLOCKS // 2, :])
-        nc.scalar.dma_start(rows[:, BLOCKS // 2 : BLOCKS, :], table_blocks[:, BLOCKS // 2 : BLOCKS, :])
-
-        gain_all = held.tile([P, D], F32, name="gain_all")
-        nc.scalar.dma_start(gain_all[:], gain.rearrange("d o -> (d o)").partition_broadcast(P))
+        gain_col = held.tile([D, 1], F32, name="gain_col")
+        nc.scalar.dma_start(gain_col[:], gain)
 
         wk_sb = held.tile([D, M], BF16, name="wk_sb")
         nc.sync.dma_start(wk_sb[:], wk)
@@ -48,39 +49,47 @@ def tile_llamamodel_kernel(tc, table, gain, wk, cosv, sinv, offs, out):
             nc.sync.dma_start(cos_col[q * HALF : (q + 1) * HALF, :], cosv)
             nc.sync.dma_start(sin_col[q * HALF : (q + 1) * HALF, :], sinv)
 
+        one = held.tile([P, 1], F32, name="one")
+        nc.vector.memset(one[:], 1.0)
+        unused = held.tile([P, 1], F32, name="unused")
+        nc.scalar.activation(unused[:], one[:], ACT.Abs_reciprocal_sqrt)
+
         wk_split = held.tile([D, 2, PAIRS], BF16, name="wk_split")
         nc.gpsimd.tensor_copy(wk_split[:], wk_sb[:].rearrange("d (q two) -> d two q", two=2))
 
-        PER_ENGINE = BLOCKS // 2
-        sumsq = held.tile([P, 2, 8], F32, name="sumsq")
+        sumsq_s = held.tile([P, PER_ENGINE], F32, name="sumsq_s")
+        sumsq_v = held.tile([P, PER_ENGINE], F32, name="sumsq_v")
         for k in range(PER_ENGINE):
-            sq_act = work.tile([P, D], F32, name="sq_act")
-            nc.scalar.activation(sq_act[:], rows[:, k, :], ACT.Square, accum_out=sumsq[:, 0, k : k + 1])
-            sq_dve = work.tile([P, D], F32, name="sq_dve")
+            sq_s = work.tile([P, D], F32, name="sq_s")
+            nc.scalar.activation(sq_s[:], rows[:, k, :], ACT.Square, accum_out=sumsq_s[:, k : k + 1])
+            sq_v = work.tile([P, D], F32, name="sq_v")
             nc.vector.scalar_tensor_tensor(
-                sq_dve[:], rows[:, PER_ENGINE + k, :], 1.0, rows[:, PER_ENGINE + k, :], MULT, MULT,
-                accum_out=sumsq[:, 1, k : k + 1],
+                sq_v[:], rows[:, PER_ENGINE + k, :], 1.0, rows[:, PER_ENGINE + k, :], MULT, MULT,
+                accum_out=sumsq_v[:, k : k + 1],
             )
-        rms = held.tile([P, 2, PER_ENGINE], F32, name="rms")
-        nc.scalar.activation(rms[:], sumsq[:, :, 0:PER_ENGINE], ACT.Sqrt, bias=EPS, scale=1.0 / D)
-        rstd = held.tile([P, BLOCKS], F32, name="rstd")
-        nc.vector.reciprocal(rstd[:], rms[:].rearrange("p e k -> p (e k)"))
+        rstd_s = held.tile([P, PER_ENGINE], F32, name="rstd_s")
+        nc.scalar.activation(rstd_s[:], sumsq_s[:], ACT.Abs_reciprocal_sqrt, bias=EPS, scale=1.0 / D)
+        rstd_v = held.tile([P, PER_ENGINE], F32, name="rstd_v")
+        nc.scalar.activation(rstd_v[:], sumsq_v[:], ACT.Abs_reciprocal_sqrt, bias=EPS, scale=1.0 / D)
 
-        xn = held.tile([P, BLOCKS, D], BF16, name="xn")
-        for t in range(BLOCKS):
-            nc.vector.scalar_tensor_tensor(
-                xn[:, t, :], rows[:, t, :], rstd[:, t : t + 1], gain_all[:], MULT, MULT
+        unit = held.tile([P, BLOCKS, D], F32, name="unit")
+        for k in range(PER_ENGINE):
+            nc.scalar.activation(unit[:, k, :], rows[:, k, :], ACT.Copy, scale=rstd_s[:, k : k + 1])
+            nc.vector.tensor_scalar(
+                unit[:, PER_ENGINE + k, :], rows[:, PER_ENGINE + k, :], rstd_v[:, k : k + 1], None, MULT
             )
 
         window = held.tile([D, V], BF16, name="window")
-        for g in range(BLOCKS // 2):
-            flipped = flip.tile([D, 2 * P], BF16, name="flipped")
-            for t in (2 * g, 2 * g + 1):
-                nc.tensor.transpose(flipped[:, (t % 2) * P : (t % 2 + 1) * P], xn[:, t, :], identity[:])
-            if g % 2 == 0:
-                nc.vector.tensor_copy(window[:, g * 2 * P : (g + 1) * 2 * P], flipped[:])
-            else:
-                nc.scalar.copy(window[:, g * 2 * P : (g + 1) * 2 * P], flipped[:])
+        for pair in range(PER_ENGINE // 2):
+            for first_block in (2 * pair, PER_ENGINE + 2 * pair):
+                flipped = flip.tile([D, 2 * P], F32, name="flipped")
+                for side in range(2):
+                    nc.tensor.transpose(flipped[:, side * P : (side + 1) * P], unit[:, first_block + side, :], identity[:])
+                xn = window[:, first_block * P : (first_block + 2) * P]
+                if first_block < PER_ENGINE:
+                    nc.scalar.activation(xn, flipped[:], ACT.Copy, scale=gain_col[:, 0:1])
+                else:
+                    nc.vector.tensor_scalar(xn, flipped[:], gain_col[:, 0:1], None, MULT)
 
         out_rows = out.rearrange("(b q half i) j -> b half q i j", b=GROUPS, q=HEADS_IN_GROUP, half=2, i=HALF)
         for b in range(GROUPS):

@@ -16,6 +16,7 @@ PER_ENGINE = BLOCKS // 2
 PAIRS = M // 2
 GROUPS = PAIRS // P
 HEADS_IN_GROUP = P // HALF
+WARM_UP = 10
 
 
 def tile_llamamodel_kernel(tc, table, gain, wk, cosv, sinv, offs, out):
@@ -23,25 +24,29 @@ def tile_llamamodel_kernel(tc, table, gain, wk, cosv, sinv, offs, out):
     with (
         tc.tile_pool(name="held", bufs=1) as held,
         tc.tile_pool(name="work", bufs=2) as work,
-        tc.psum_pool(name="flip", bufs=4) as flip,
+        tc.psum_pool(name="idle", bufs=1) as idle,
+        tc.psum_pool(name="flip", bufs=3) as flip,
         tc.psum_pool(name="keys", bufs=2) as keys,
     ):
-        identity = held.tile([P, P], F32, name="identity")
-        make_identity(nc, identity[:])
+        zeros = held.tile([P, N], BF16, name="zeros")
+        nc.gpsimd.memset(zeros[:], 0.0)
+        discarded = idle.tile([P, N], F32, name="discarded")
+        for repeat in range(WARM_UP):
+            nc.tensor.matmul(discarded[:], zeros[:, 0:P], zeros[:], start=True, stop=True)
 
         rows = held.tile([P, BLOCKS, D], BF16, name="rows")
         table_blocks = table.rearrange("(t p) d -> p t d", p=P)
         nc.sync.dma_start(rows[:, 0:PER_ENGINE, :], table_blocks[:, 0:PER_ENGINE, :])
         nc.scalar.dma_start(rows[:, PER_ENGINE:BLOCKS, :], table_blocks[:, PER_ENGINE:BLOCKS, :])
 
-        offsets = held.tile([P, N // 16], U16, name="offsets")
-        nc.sync.dma_start(offsets[:], offs)
-
-        gain_col = held.tile([D, 1], F32, name="gain_col")
-        nc.scalar.dma_start(gain_col[:], gain)
+        gain_all = held.tile([P, D], F32, name="gain_all")
+        nc.sync.dma_start(gain_all[:], gain.rearrange("d o -> (d o)").partition_broadcast(P))
 
         wk_sb = held.tile([D, M], BF16, name="wk_sb")
         nc.sync.dma_start(wk_sb[:], wk)
+
+        offsets = held.tile([P, N // 16], U16, name="offsets")
+        nc.sync.dma_start(offsets[:], offs)
 
         cos_col = held.tile([P, 1], F32, name="cos_col")
         sin_col = held.tile([P, 1], F32, name="sin_col")
@@ -49,13 +54,18 @@ def tile_llamamodel_kernel(tc, table, gain, wk, cosv, sinv, offs, out):
             nc.sync.dma_start(cos_col[q * HALF : (q + 1) * HALF, :], cosv)
             nc.sync.dma_start(sin_col[q * HALF : (q + 1) * HALF, :], sinv)
 
+        identity = held.tile([P, P], BF16, name="identity")
+        make_identity(nc, identity[:])
+
         one = held.tile([P, 1], F32, name="one")
-        nc.vector.memset(one[:], 1.0)
+        nc.gpsimd.memset(one[:], 1.0)
         unused = held.tile([P, 1], F32, name="unused")
         nc.scalar.activation(unused[:], one[:], ACT.Abs_reciprocal_sqrt)
 
-        wk_split = held.tile([D, 2, PAIRS], BF16, name="wk_split")
-        nc.gpsimd.tensor_copy(wk_split[:], wk_sb[:].rearrange("d (q two) -> d two q", two=2))
+        wk_split = held.tile([D, GROUPS, 2, P], BF16, name="wk_split")
+        wk_pairs = wk_sb[:].rearrange("d (b q two) -> d b two q", b=GROUPS, two=2)
+        for b in range(GROUPS):
+            nc.gpsimd.tensor_copy(wk_split[:, b, :, :], wk_pairs[:, b, :, :])
 
         sumsq_s = held.tile([P, PER_ENGINE], F32, name="sumsq_s")
         sumsq_v = held.tile([P, PER_ENGINE], F32, name="sumsq_v")
@@ -67,39 +77,29 @@ def tile_llamamodel_kernel(tc, table, gain, wk, cosv, sinv, offs, out):
                 sq_v[:], rows[:, PER_ENGINE + k, :], 1.0, rows[:, PER_ENGINE + k, :], MULT, MULT,
                 accum_out=sumsq_v[:, k : k + 1],
             )
-        rstd_s = held.tile([P, PER_ENGINE], F32, name="rstd_s")
-        nc.scalar.activation(rstd_s[:], sumsq_s[:], ACT.Abs_reciprocal_sqrt, bias=EPS, scale=1.0 / D)
-        rstd_v = held.tile([P, PER_ENGINE], F32, name="rstd_v")
-        nc.scalar.activation(rstd_v[:], sumsq_v[:], ACT.Abs_reciprocal_sqrt, bias=EPS, scale=1.0 / D)
+        rstd = held.tile([P, BLOCKS], F32, name="rstd")
+        nc.scalar.activation(rstd[:, 0:PER_ENGINE], sumsq_s[:], ACT.Abs_reciprocal_sqrt, bias=EPS, scale=1.0 / D)
+        nc.scalar.activation(rstd[:, PER_ENGINE:BLOCKS], sumsq_v[:], ACT.Abs_reciprocal_sqrt, bias=EPS, scale=1.0 / D)
 
-        unit = held.tile([P, BLOCKS, D], F32, name="unit")
-        for k in range(PER_ENGINE):
-            nc.scalar.activation(unit[:, k, :], rows[:, k, :], ACT.Copy, scale=rstd_s[:, k : k + 1])
-            nc.vector.tensor_scalar(
-                unit[:, PER_ENGINE + k, :], rows[:, PER_ENGINE + k, :], rstd_v[:, k : k + 1], None, MULT
-            )
-
+        xn = held.tile([P, BLOCKS, D], BF16, name="xn")
         window = held.tile([D, V], BF16, name="window")
-        for pair in range(PER_ENGINE // 2):
-            for first_block in (2 * pair, PER_ENGINE + 2 * pair):
-                flipped = flip.tile([D, 2 * P], F32, name="flipped")
-                for side in range(2):
-                    nc.tensor.transpose(flipped[:, side * P : (side + 1) * P], unit[:, first_block + side, :], identity[:])
-                xn = window[:, first_block * P : (first_block + 2) * P]
-                if first_block < PER_ENGINE:
-                    nc.scalar.activation(xn, flipped[:], ACT.Copy, scale=gain_col[:, 0:1])
-                else:
-                    nc.vector.tensor_scalar(xn, flipped[:], gain_col[:, 0:1], None, MULT)
+        for first_block in range(0, BLOCKS, 2):
+            flipped = flip.tile([D, 2 * P], BF16, name="flipped")
+            for side in range(2):
+                t = first_block + side
+                nc.vector.scalar_tensor_tensor(xn[:, t, :], rows[:, t, :], rstd[:, t : t + 1], gain_all[:], MULT, MULT)
+                nc.tensor.transpose(flipped[:, side * P : (side + 1) * P], xn[:, t, :], identity[:])
+            nc.scalar.copy(window[:, first_block * P : (first_block + 2) * P], flipped[:])
 
         out_rows = out.rearrange("(b q half i) j -> b half q i j", b=GROUPS, q=HEADS_IN_GROUP, half=2, i=HALF)
         for b in range(GROUPS):
             k_odd = keys.tile([P, N], F32, name="k_odd")
             nc.tensor.matmul(
-                k_odd[:], wk_split[:, 1, b * P : (b + 1) * P], window[:].indirect(offsets[:]), start=True, stop=True
+                k_odd[:], wk_split[:, b, 1, :], window[:].indirect(offsets[:]), start=True, stop=True
             )
             k_even = keys.tile([P, N], F32, name="k_even")
             nc.tensor.matmul(
-                k_even[:], wk_split[:, 0, b * P : (b + 1) * P], window[:].indirect(offsets[:]), start=True, stop=True
+                k_even[:], wk_split[:, b, 0, :], window[:].indirect(offsets[:]), start=True, stop=True
             )
             odd_sin = work.tile([P, N], F32, name="odd_sin")
             nc.scalar.activation(odd_sin[:], k_odd[:], ACT.Copy, scale=sin_col[:, 0:1])

@@ -16,7 +16,6 @@ PER_ENGINE = BLOCKS // 2
 PAIRS = M // 2
 GROUPS = PAIRS // P
 HEADS_IN_GROUP = P // HALF
-WARM_UP = 10
 
 
 def tile_llamamodel_kernel(tc, table, gain, wk, cosv, sinv, offs, out):
@@ -24,29 +23,25 @@ def tile_llamamodel_kernel(tc, table, gain, wk, cosv, sinv, offs, out):
     with (
         tc.tile_pool(name="held", bufs=1) as held,
         tc.tile_pool(name="work", bufs=2) as work,
-        tc.psum_pool(name="idle", bufs=1) as idle,
-        tc.psum_pool(name="flip", bufs=3) as flip,
+        tc.psum_pool(name="flip", bufs=4) as flip,
         tc.psum_pool(name="keys", bufs=2) as keys,
     ):
-        zeros = held.tile([P, N], BF16, name="zeros")
-        nc.gpsimd.memset(zeros[:], 0.0)
-        discarded = idle.tile([P, N], F32, name="discarded")
-        for repeat in range(WARM_UP):
-            nc.tensor.matmul(discarded[:], zeros[:, 0:P], zeros[:], start=True, stop=True)
+        identity = held.tile([P, P], F32, name="identity")
+        make_identity(nc, identity[:])
 
         rows = held.tile([P, BLOCKS, D], BF16, name="rows")
         table_blocks = table.rearrange("(t p) d -> p t d", p=P)
         nc.sync.dma_start(rows[:, 0:PER_ENGINE, :], table_blocks[:, 0:PER_ENGINE, :])
         nc.scalar.dma_start(rows[:, PER_ENGINE:BLOCKS, :], table_blocks[:, PER_ENGINE:BLOCKS, :])
 
-        gain_all = held.tile([P, D], F32, name="gain_all")
-        nc.sync.dma_start(gain_all[:], gain.rearrange("d o -> (d o)").partition_broadcast(P))
+        offsets = held.tile([P, N // 16], U16, name="offsets")
+        nc.sync.dma_start(offsets[:], offs)
+
+        gain_col = held.tile([D, 1], F32, name="gain_col")
+        nc.scalar.dma_start(gain_col[:], gain)
 
         wk_sb = held.tile([D, M], BF16, name="wk_sb")
         nc.sync.dma_start(wk_sb[:], wk)
-
-        offsets = held.tile([P, N // 16], U16, name="offsets")
-        nc.sync.dma_start(offsets[:], offs)
 
         cos_col = held.tile([P, 1], F32, name="cos_col")
         sin_col = held.tile([P, 1], F32, name="sin_col")
@@ -54,18 +49,10 @@ def tile_llamamodel_kernel(tc, table, gain, wk, cosv, sinv, offs, out):
             nc.sync.dma_start(cos_col[q * HALF : (q + 1) * HALF, :], cosv)
             nc.sync.dma_start(sin_col[q * HALF : (q + 1) * HALF, :], sinv)
 
-        identity = held.tile([P, P], BF16, name="identity")
-        make_identity(nc, identity[:])
-
         one = held.tile([P, 1], F32, name="one")
-        nc.gpsimd.memset(one[:], 1.0)
+        nc.vector.memset(one[:], 1.0)
         unused = held.tile([P, 1], F32, name="unused")
         nc.scalar.activation(unused[:], one[:], ACT.Abs_reciprocal_sqrt)
-
-        wk_split = held.tile([D, GROUPS, 2, P], BF16, name="wk_split")
-        wk_pairs = wk_sb[:].rearrange("d (b q two) -> d b two q", b=GROUPS, two=2)
-        for b in range(GROUPS):
-            nc.gpsimd.tensor_copy(wk_split[:, b, :, :], wk_pairs[:, b, :, :])
 
         sumsq_s = held.tile([P, PER_ENGINE], F32, name="sumsq_s")
         sumsq_v = held.tile([P, PER_ENGINE], F32, name="sumsq_v")
@@ -77,19 +64,34 @@ def tile_llamamodel_kernel(tc, table, gain, wk, cosv, sinv, offs, out):
                 sq_v[:], rows[:, PER_ENGINE + k, :], 1.0, rows[:, PER_ENGINE + k, :], MULT, MULT,
                 accum_out=sumsq_v[:, k : k + 1],
             )
-        rstd = held.tile([P, BLOCKS], F32, name="rstd")
-        nc.scalar.activation(rstd[:, 0:PER_ENGINE], sumsq_s[:], ACT.Abs_reciprocal_sqrt, bias=EPS, scale=1.0 / D)
-        nc.scalar.activation(rstd[:, PER_ENGINE:BLOCKS], sumsq_v[:], ACT.Abs_reciprocal_sqrt, bias=EPS, scale=1.0 / D)
+        rstd_s = held.tile([P, PER_ENGINE], F32, name="rstd_s")
+        nc.scalar.activation(rstd_s[:], sumsq_s[:], ACT.Abs_reciprocal_sqrt, bias=EPS, scale=1.0 / D)
+        rstd_v = held.tile([P, PER_ENGINE], F32, name="rstd_v")
+        nc.scalar.activation(rstd_v[:], sumsq_v[:], ACT.Abs_reciprocal_sqrt, bias=EPS, scale=1.0 / D)
 
-        xn = held.tile([P, BLOCKS, D], BF16, name="xn")
+        unit = held.tile([P, BLOCKS, D], F32, name="unit")
+        for k in range(PER_ENGINE):
+            nc.scalar.activation(unit[:, k, :], rows[:, k, :], ACT.Copy, scale=rstd_s[:, k : k + 1])
+            nc.vector.tensor_scalar(
+                unit[:, PER_ENGINE + k, :], rows[:, PER_ENGINE + k, :], rstd_v[:, k : k + 1], None, MULT
+            )
+
+        wk_split = held.tile([D, GROUPS, 2, P], BF16, name="wk_split")
+        wk_pairs = wk_sb[:].rearrange("d (b q two) -> d b two q", b=GROUPS, two=2)
+        nc.scalar.copy(wk_split[:, 0, :, :], wk_pairs[:, 0, :, :])
+        nc.vector.tensor_copy(wk_split[:, 1, :, :], wk_pairs[:, 1, :, :])
+
         window = held.tile([D, V], BF16, name="window")
-        for first_block in range(0, BLOCKS, 2):
-            flipped = flip.tile([D, 2 * P], BF16, name="flipped")
-            for side in range(2):
-                t = first_block + side
-                nc.vector.scalar_tensor_tensor(xn[:, t, :], rows[:, t, :], rstd[:, t : t + 1], gain_all[:], MULT, MULT)
-                nc.tensor.transpose(flipped[:, side * P : (side + 1) * P], xn[:, t, :], identity[:])
-            nc.scalar.copy(window[:, first_block * P : (first_block + 2) * P], flipped[:])
+        for pair in range(PER_ENGINE // 2):
+            for first_block in (2 * pair, PER_ENGINE + 2 * pair):
+                flipped = flip.tile([D, 2 * P], F32, name="flipped")
+                for side in range(2):
+                    nc.tensor.transpose(flipped[:, side * P : (side + 1) * P], unit[:, first_block + side, :], identity[:])
+                xn = window[:, first_block * P : (first_block + 2) * P]
+                if first_block < PER_ENGINE:
+                    nc.scalar.activation(xn, flipped[:], ACT.Copy, scale=gain_col[:, 0:1])
+                else:
+                    nc.vector.tensor_scalar(xn, flipped[:], gain_col[:, 0:1], None, MULT)
 
         out_rows = out.rearrange("(b q half i) j -> b half q i j", b=GROUPS, q=HEADS_IN_GROUP, half=2, i=HALF)
         for b in range(GROUPS):

@@ -16,6 +16,7 @@ PER_ENGINE = BLOCKS // 2
 PAIRS = M // 2
 GROUPS = PAIRS // P
 HEADS_IN_GROUP = P // HALF
+WARM_UP = 8
 
 
 def tile_llamamodel_kernel(tc, table, gain, wk, cosv, sinv, offs, out):
@@ -23,7 +24,8 @@ def tile_llamamodel_kernel(tc, table, gain, wk, cosv, sinv, offs, out):
     with (
         tc.tile_pool(name="held", bufs=1) as held,
         tc.tile_pool(name="work", bufs=2) as work,
-        tc.psum_pool(name="flip", bufs=4) as flip,
+        tc.psum_pool(name="idle", bufs=1) as idle,
+        tc.psum_pool(name="flip", bufs=3) as flip,
         tc.psum_pool(name="keys", bufs=2) as keys,
     ):
         identity = held.tile([P, P], F32, name="identity")
@@ -54,6 +56,15 @@ def tile_llamamodel_kernel(tc, table, gain, wk, cosv, sinv, offs, out):
         unused = held.tile([P, 1], F32, name="unused")
         nc.scalar.activation(unused[:], one[:], ACT.Abs_reciprocal_sqrt)
 
+        ones = held.tile([P, N], BF16, name="ones")
+        nc.vector.memset(ones[:], 1.0)
+        discarded = idle.tile([P, N], F32, name="discarded")
+        for repeat in range(WARM_UP):
+            nc.tensor.matmul(discarded[:], ones[:, 0:P], ones[:], start=True, stop=True)
+
+        wk_split = held.tile([D, 2, PAIRS], BF16, name="wk_split")
+        nc.gpsimd.tensor_copy(wk_split[:], wk_sb[:].rearrange("d (q two) -> d two q", two=2))
+
         sumsq_s = held.tile([P, PER_ENGINE], F32, name="sumsq_s")
         sumsq_v = held.tile([P, PER_ENGINE], F32, name="sumsq_v")
         for k in range(PER_ENGINE):
@@ -76,11 +87,6 @@ def tile_llamamodel_kernel(tc, table, gain, wk, cosv, sinv, offs, out):
                 unit[:, PER_ENGINE + k, :], rows[:, PER_ENGINE + k, :], rstd_v[:, k : k + 1], None, MULT
             )
 
-        wk_split = held.tile([D, GROUPS, 2, P], BF16, name="wk_split")
-        wk_pairs = wk_sb[:].rearrange("d (b q two) -> d b two q", b=GROUPS, two=2)
-        nc.scalar.copy(wk_split[:, 0, :, :], wk_pairs[:, 0, :, :])
-        nc.vector.tensor_copy(wk_split[:, 1, :, :], wk_pairs[:, 1, :, :])
-
         window = held.tile([D, V], BF16, name="window")
         for pair in range(PER_ENGINE // 2):
             for first_block in (2 * pair, PER_ENGINE + 2 * pair):
@@ -97,11 +103,11 @@ def tile_llamamodel_kernel(tc, table, gain, wk, cosv, sinv, offs, out):
         for b in range(GROUPS):
             k_odd = keys.tile([P, N], F32, name="k_odd")
             nc.tensor.matmul(
-                k_odd[:], wk_split[:, b, 1, :], window[:].indirect(offsets[:]), start=True, stop=True
+                k_odd[:], wk_split[:, 1, b * P : (b + 1) * P], window[:].indirect(offsets[:]), start=True, stop=True
             )
             k_even = keys.tile([P, N], F32, name="k_even")
             nc.tensor.matmul(
-                k_even[:], wk_split[:, b, 0, :], window[:].indirect(offsets[:]), start=True, stop=True
+                k_even[:], wk_split[:, 0, b * P : (b + 1) * P], window[:].indirect(offsets[:]), start=True, stop=True
             )
             odd_sin = work.tile([P, N], F32, name="odd_sin")
             nc.scalar.activation(odd_sin[:], k_odd[:], ACT.Copy, scale=sin_col[:, 0:1])

@@ -16,7 +16,6 @@ PER_ENGINE = BLOCKS // 2
 PAIRS = M // 2
 GROUPS = PAIRS // P
 HEADS_IN_GROUP = P // HALF
-WARM_UP = 8
 
 
 def tile_llamamodel_kernel(tc, table, gain, wk, cosv, sinv, offs, out):
@@ -24,8 +23,7 @@ def tile_llamamodel_kernel(tc, table, gain, wk, cosv, sinv, offs, out):
     with (
         tc.tile_pool(name="held", bufs=1) as held,
         tc.tile_pool(name="work", bufs=2) as work,
-        tc.psum_pool(name="idle", bufs=1) as idle,
-        tc.psum_pool(name="flip", bufs=3) as flip,
+        tc.psum_pool(name="flip", bufs=4) as flip,
         tc.psum_pool(name="keys", bufs=2) as keys,
     ):
         identity = held.tile([P, P], F32, name="identity")
@@ -42,25 +40,19 @@ def tile_llamamodel_kernel(tc, table, gain, wk, cosv, sinv, offs, out):
         gain_col = held.tile([D, 1], F32, name="gain_col")
         nc.scalar.dma_start(gain_col[:], gain)
 
-        wk_sb = held.tile([D, M], BF16, name="wk_sb")
-        nc.sync.dma_start(wk_sb[:], wk)
-
         cos_col = held.tile([P, 1], F32, name="cos_col")
         sin_col = held.tile([P, 1], F32, name="sin_col")
         for q in range(HEADS_IN_GROUP):
             nc.sync.dma_start(cos_col[q * HALF : (q + 1) * HALF, :], cosv)
             nc.sync.dma_start(sin_col[q * HALF : (q + 1) * HALF, :], sinv)
 
+        wk_sb = held.tile([D, M], BF16, name="wk_sb")
+        nc.sync.dma_start(wk_sb[:], wk)
+
         one = held.tile([P, 1], F32, name="one")
         nc.vector.memset(one[:], 1.0)
         unused = held.tile([P, 1], F32, name="unused")
         nc.scalar.activation(unused[:], one[:], ACT.Abs_reciprocal_sqrt)
-
-        ones = held.tile([P, N], BF16, name="ones")
-        nc.vector.memset(ones[:], 1.0)
-        discarded = idle.tile([P, N], F32, name="discarded")
-        for repeat in range(WARM_UP):
-            nc.tensor.matmul(discarded[:], ones[:, 0:P], ones[:], start=True, stop=True)
 
         wk_split = held.tile([D, 2, PAIRS], BF16, name="wk_split")
         nc.gpsimd.tensor_copy(wk_split[:], wk_sb[:].rearrange("d (q two) -> d two q", two=2))

@@ -30,9 +30,10 @@ def tile_llamamodel_kernel(tc, table, gain, wk, cosv, sinv, offs, out):
         make_identity(nc, identity[:])
 
         rows = held.tile([P, BLOCKS, D], BF16, name="rows")
-        table_blocks = table.rearrange("(t p) d -> p t d", p=P)
-        nc.sync.dma_start(rows[:, 0:PER_ENGINE, :], table_blocks[:, 0:PER_ENGINE, :])
-        nc.scalar.dma_start(rows[:, PER_ENGINE:BLOCKS, :], table_blocks[:, PER_ENGINE:BLOCKS, :])
+        table_runs = table.rearrange("(g p side) d -> p g (side d)", p=P, side=2)
+        rows_runs = rows[:].rearrange("p (g side) d -> p g (side d)", side=2)
+        nc.sync.dma_start(rows_runs[:, 0 : PER_ENGINE // 2, :], table_runs[:, 0 : PER_ENGINE // 2, :])
+        nc.scalar.dma_start(rows_runs[:, PER_ENGINE // 2 : PER_ENGINE, :], table_runs[:, PER_ENGINE // 2 : PER_ENGINE, :])
 
         offsets = held.tile([P, N // 16], U16, name="offsets")
         nc.sync.dma_start(offsets[:], offs)
@@ -40,14 +41,14 @@ def tile_llamamodel_kernel(tc, table, gain, wk, cosv, sinv, offs, out):
         gain_col = held.tile([D, 1], F32, name="gain_col")
         nc.scalar.dma_start(gain_col[:], gain)
 
+        wk_sb = held.tile([D, M], BF16, name="wk_sb")
+        nc.sync.dma_start(wk_sb[:], wk)
+
         cos_col = held.tile([P, 1], F32, name="cos_col")
         sin_col = held.tile([P, 1], F32, name="sin_col")
         for q in range(HEADS_IN_GROUP):
             nc.sync.dma_start(cos_col[q * HALF : (q + 1) * HALF, :], cosv)
             nc.sync.dma_start(sin_col[q * HALF : (q + 1) * HALF, :], sinv)
-
-        wk_sb = held.tile([D, M], BF16, name="wk_sb")
-        nc.sync.dma_start(wk_sb[:], wk)
 
         one = held.tile([P, 1], F32, name="one")
         nc.vector.memset(one[:], 1.0)
@@ -85,11 +86,12 @@ def tile_llamamodel_kernel(tc, table, gain, wk, cosv, sinv, offs, out):
                 flipped = flip.tile([D, 2 * P], F32, name="flipped")
                 for side in range(2):
                     nc.tensor.transpose(flipped[:, side * P : (side + 1) * P], unit[:, first_block + side, :], identity[:])
-                xn = window[:, first_block * P : (first_block + 2) * P]
+                xn = window[:, first_block * P : (first_block + 2) * P].rearrange("d (p side) -> d p side", side=2)
+                in_turn = flipped[:].rearrange("d (side p) -> d p side", side=2)
                 if first_block < PER_ENGINE:
-                    nc.scalar.activation(xn, flipped[:], ACT.Copy, scale=gain_col[:, 0:1])
+                    nc.scalar.activation(xn, in_turn, ACT.Copy, scale=gain_col[:, 0:1])
                 else:
-                    nc.vector.tensor_scalar(xn, flipped[:], gain_col[:, 0:1], None, MULT)
+                    nc.vector.tensor_scalar(xn, in_turn, gain_col[:, 0:1], None, MULT)
 
         out_rows = out.rearrange("(b q half i) j -> b half q i j", b=GROUPS, q=HEADS_IN_GROUP, half=2, i=HALF)
         for b in range(GROUPS):

@@ -47,8 +47,8 @@ def tile_llamamodel_kernel(tc, table, gain, wk, cosv, sinv, offs, out):
         cos_col = held.tile([P, 1], F32, name="cos_col")
         sin_col = held.tile([P, 1], F32, name="sin_col")
         for q in range(HEADS_IN_GROUP):
-            nc.sync.dma_start(cos_col[q * HALF : (q + 1) * HALF, :], cosv)
-            nc.sync.dma_start(sin_col[q * HALF : (q + 1) * HALF, :], sinv)
+            nc.sync.dma_start(cos_col[q:P:HEADS_IN_GROUP, :], cosv)
+            nc.sync.dma_start(sin_col[q:P:HEADS_IN_GROUP, :], sinv)
 
         one = held.tile([P, 1], F32, name="one")
         nc.vector.memset(one[:], 1.0)
@@ -56,7 +56,11 @@ def tile_llamamodel_kernel(tc, table, gain, wk, cosv, sinv, offs, out):
         nc.scalar.activation(unused[:], one[:], ACT.Abs_reciprocal_sqrt)
 
         wk_split = held.tile([D, 2, PAIRS], BF16, name="wk_split")
-        nc.gpsimd.tensor_copy(wk_split[:], wk_sb[:].rearrange("d (q two) -> d two q", two=2))
+        wk_pairs = wk_sb[:].rearrange("d (b q i two) -> d two b i q", b=GROUPS, q=HEADS_IN_GROUP, two=2)
+        for two in range(2):
+            nc.gpsimd.tensor_copy(
+                wk_split[:, two, :].rearrange("d (b i q) -> d b i q", b=GROUPS, q=HEADS_IN_GROUP), wk_pairs[:, two]
+            )
 
         sumsq_s = held.tile([P, PER_ENGINE], F32, name="sumsq_s")
         sumsq_v = held.tile([P, PER_ENGINE], F32, name="sumsq_v")
@@ -113,4 +117,4 @@ def tile_llamamodel_kernel(tc, table, gain, wk, cosv, sinv, offs, out):
             nc.vector.scalar_tensor_tensor(second[:], k_even[:], sin_col[:, 0:1], odd_cos[:], MULT, ADD)
             for half, rotated in enumerate((first, second)):
                 for q in range(HEADS_IN_GROUP):
-                    nc.sync.dma_start(out_rows[b, half, q], rotated[q * HALF : (q + 1) * HALF, :])
+                    nc.sync.dma_start(out_rows[b, half, q], rotated[q:P:HEADS_IN_GROUP, :])

@@ -32,14 +32,15 @@ def tile_llamamodel_kernel(tc, table, gain, wk, cosv, sinv, offs, out):
         rows = held.tile([P, BLOCKS, D], BF16, name="rows")
         table_runs = table.rearrange("(g p side) d -> p g (side d)", p=P, side=2)
         rows_runs = rows[:].rearrange("p (g side) d -> p g (side d)", side=2)
-        nc.sync.dma_start(rows_runs[:, 0 : PER_ENGINE // 2, :], table_runs[:, 0 : PER_ENGINE // 2, :])
-        nc.scalar.dma_start(rows_runs[:, PER_ENGINE // 2 : PER_ENGINE, :], table_runs[:, PER_ENGINE // 2 : PER_ENGINE, :])
+        for pair in range(PER_ENGINE // 2):
+            for g in (pair, PER_ENGINE // 2 + pair):
+                nc.sync.dma_start(rows_runs[:, g : g + 1, :], table_runs[:, g : g + 1, :])
 
         offsets = held.tile([P, N // 16], U16, name="offsets")
         nc.sync.dma_start(offsets[:], offs)
 
         gain_col = held.tile([D, 1], F32, name="gain_col")
-        nc.scalar.dma_start(gain_col[:], gain)
+        nc.sync.dma_start(gain_col[:], gain)
 
         wk_sb = held.tile([D, M], BF16, name="wk_sb")
         nc.sync.dma_start(wk_sb[:], wk)

@@ -98,7 +98,7 @@ def tile_llamamodel_kernel(tc, table, gain, wk, cosv, sinv, offs, out):
                 else:
                     nc.vector.tensor_scalar(xn, in_turn, gain_col[:, 0:1], None, MULT)
 
-        out_rows = out.rearrange("(b q half i) j -> b half q i j", b=GROUPS, q=HEADS_IN_GROUP, half=2, i=HALF)
+        out_rows = out.rearrange("(b q half i) j -> b half i q j", b=GROUPS, q=HEADS_IN_GROUP, half=2, i=HALF)
         for b in range(GROUPS):
             k_odd = keys.tile([P, N], F32, name="k_odd")
             nc.tensor.matmul(
@@ -117,5 +117,4 @@ def tile_llamamodel_kernel(tc, table, gain, wk, cosv, sinv, offs, out):
             second = work.tile([P, N], F32, name="second")
             nc.vector.scalar_tensor_tensor(second[:], k_even[:], sin_col[:, 0:1], odd_cos[:], MULT, ADD)
             for half, rotated in enumerate((first, second)):
-                for q in range(HEADS_IN_GROUP):
-                    nc.sync.dma_start(out_rows[b, half, q], rotated[q:P:HEADS_IN_GROUP, :])
+                nc.sync.dma_start(out_rows[b, half], rotated[:])

@@ -12,7 +12,7 @@ MULT, ADD, SUBTRACT = mybir.AluOpType.mult, mybir.AluOpType.add, mybir.AluOpType
 ACT = mybir.ActivationFunctionType
 
 BLOCKS = V // P
-PER_ENGINE = BLOCKS // 2
+PAIRS_OF_BLOCKS = BLOCKS // 2
 PAIRS = M // 2
 GROUPS = PAIRS // P
 HEADS_IN_GROUP = P // HALF
@@ -32,9 +32,8 @@ def tile_llamamodel_kernel(tc, table, gain, wk, cosv, sinv, offs, out):
         rows = held.tile([P, BLOCKS, D], BF16, name="rows")
         table_runs = table.rearrange("(g p side) d -> p g (side d)", p=P, side=2)
         rows_runs = rows[:].rearrange("p (g side) d -> p g (side d)", side=2)
-        for pair in range(PER_ENGINE // 2):
-            for g in (pair, PER_ENGINE // 2 + pair):
-                nc.sync.dma_start(rows_runs[:, g : g + 1, :], table_runs[:, g : g + 1, :])
+        for g in range(PAIRS_OF_BLOCKS):
+            nc.sync.dma_start(rows_runs[:, g : g + 1, :], table_runs[:, g : g + 1, :])
 
         offsets = held.tile([P, N // 16], U16, name="offsets")
         nc.sync.dma_start(offsets[:], offs)
@@ -47,9 +46,8 @@ def tile_llamamodel_kernel(tc, table, gain, wk, cosv, sinv, offs, out):
 
         cos_col = held.tile([P, 1], F32, name="cos_col")
         sin_col = held.tile([P, 1], F32, name="sin_col")
-        for q in range(HEADS_IN_GROUP):
-            nc.sync.dma_start(cos_col[q:P:HEADS_IN_GROUP, :], cosv)
-            nc.sync.dma_start(sin_col[q:P:HEADS_IN_GROUP, :], sinv)
+        nc.sync.dma_start(cos_col[:], cosv.unsqueeze(1).broadcast_to([HALF, HEADS_IN_GROUP, 1]))
+        nc.sync.dma_start(sin_col[:], sinv.unsqueeze(1).broadcast_to([HALF, HEADS_IN_GROUP, 1]))
 
         one = held.tile([P, 1], F32, name="one")
         nc.vector.memset(one[:], 1.0)
@@ -63,40 +61,43 @@ def tile_llamamodel_kernel(tc, table, gain, wk, cosv, sinv, offs, out):
                 wk_split[:, two, :].rearrange("d (b i q) -> d b i q", b=GROUPS, q=HEADS_IN_GROUP), wk_pairs[:, two]
             )
 
-        sumsq_s = held.tile([P, PER_ENGINE], F32, name="sumsq_s")
-        sumsq_v = held.tile([P, PER_ENGINE], F32, name="sumsq_v")
-        for k in range(PER_ENGINE):
+        sumsq = held.tile([P, BLOCKS], F32, name="sumsq")
+        rstd = held.tile([P, BLOCKS], F32, name="rstd")
+        unit = held.tile([P, BLOCKS, D], F32, name="unit")
+        window = held.tile([D, V], BF16, name="window")
+        flipped_pairs = []
+
+        def normalise_and_flip(g):
+            k_s, k_v = 2 * g, 2 * g + 1
             sq_s = work.tile([P, D], F32, name="sq_s")
-            nc.scalar.activation(sq_s[:], rows[:, k, :], ACT.Square, accum_out=sumsq_s[:, k : k + 1])
+            nc.scalar.activation(sq_s[:], rows[:, k_s, :], ACT.Square, accum_out=sumsq[:, k_s : k_s + 1])
             sq_v = work.tile([P, D], F32, name="sq_v")
             nc.vector.scalar_tensor_tensor(
-                sq_v[:], rows[:, PER_ENGINE + k, :], 1.0, rows[:, PER_ENGINE + k, :], MULT, MULT,
-                accum_out=sumsq_v[:, k : k + 1],
+                sq_v[:], rows[:, k_v, :], 1.0, rows[:, k_v, :], MULT, MULT, accum_out=sumsq[:, k_v : k_v + 1]
             )
-        rstd_s = held.tile([P, PER_ENGINE], F32, name="rstd_s")
-        nc.scalar.activation(rstd_s[:], sumsq_s[:], ACT.Abs_reciprocal_sqrt, bias=EPS, scale=1.0 / D)
-        rstd_v = held.tile([P, PER_ENGINE], F32, name="rstd_v")
-        nc.scalar.activation(rstd_v[:], sumsq_v[:], ACT.Abs_reciprocal_sqrt, bias=EPS, scale=1.0 / D)
-
-        unit = held.tile([P, BLOCKS, D], F32, name="unit")
-        for k in range(PER_ENGINE):
-            nc.scalar.activation(unit[:, k, :], rows[:, k, :], ACT.Copy, scale=rstd_s[:, k : k + 1])
-            nc.vector.tensor_scalar(
-                unit[:, PER_ENGINE + k, :], rows[:, PER_ENGINE + k, :], rstd_v[:, k : k + 1], None, MULT
+            nc.scalar.activation(
+                rstd[:, k_s : k_v + 1], sumsq[:, k_s : k_v + 1], ACT.Abs_reciprocal_sqrt, bias=EPS, scale=1.0 / D
             )
+            nc.scalar.activation(unit[:, k_s, :], rows[:, k_s, :], ACT.Copy, scale=rstd[:, k_s : k_s + 1])
+            nc.vector.tensor_scalar(unit[:, k_v, :], rows[:, k_v, :], rstd[:, k_v : k_v + 1], None, MULT)
+            flipped = flip.tile([D, 2 * P], F32, name="flipped")
+            for side in range(2):
+                nc.tensor.transpose(flipped[:, side * P : (side + 1) * P], unit[:, 2 * g + side, :], identity[:])
+            flipped_pairs.append(flipped)
 
-        window = held.tile([D, V], BF16, name="window")
-        for pair in range(PER_ENGINE // 2):
-            for first_block in (2 * pair, PER_ENGINE + 2 * pair):
-                flipped = flip.tile([D, 2 * P], F32, name="flipped")
-                for side in range(2):
-                    nc.tensor.transpose(flipped[:, side * P : (side + 1) * P], unit[:, first_block + side, :], identity[:])
-                xn = window[:, first_block * P : (first_block + 2) * P].rearrange("d (p side) -> d p side", side=2)
-                in_turn = flipped[:].rearrange("d (side p) -> d p side", side=2)
-                if first_block < PER_ENGINE:
-                    nc.scalar.activation(xn, in_turn, ACT.Copy, scale=gain_col[:, 0:1])
-                else:
-                    nc.vector.tensor_scalar(xn, in_turn, gain_col[:, 0:1], None, MULT)
+        def copy_out(g):
+            xn = window[:, 2 * g * P : (2 * g + 2) * P].rearrange("d (p side) -> d p side", side=2)
+            in_turn = flipped_pairs[g][:].rearrange("d (side p) -> d p side", side=2)
+            if g % 2 == 0:
+                nc.scalar.activation(xn, in_turn, ACT.Copy, scale=gain_col[:, 0:1])
+            else:
+                nc.vector.tensor_scalar(xn, in_turn, gain_col[:, 0:1], None, MULT)
+
+        for g in range(PAIRS_OF_BLOCKS + 1):
+            if g < PAIRS_OF_BLOCKS:
+                normalise_and_flip(g)
+            if g >= 1:
+                copy_out(g - 1)
 
         out_rows = out.rearrange("(b q half i) j -> b half i q j", b=GROUPS, q=HEADS_IN_GROUP, half=2, i=HALF)
         for b in range(GROUPS):

@@ -35,14 +35,14 @@ def tile_llamamodel_kernel(tc, table, gain, wk, cosv, sinv, offs, out):
         for g in range(PAIRS_OF_BLOCKS):
             nc.sync.dma_start(rows_runs[:, g : g + 1, :], table_runs[:, g : g + 1, :])
 
+        wk_sb = held.tile([D, M], BF16, name="wk_sb")
+        nc.sync.dma_start(wk_sb[:], wk)
+
         offsets = held.tile([P, N // 16], U16, name="offsets")
         nc.sync.dma_start(offsets[:], offs)
 
         gain_col = held.tile([D, 1], F32, name="gain_col")
         nc.sync.dma_start(gain_col[:], gain)
-
-        wk_sb = held.tile([D, M], BF16, name="wk_sb")
-        nc.sync.dma_start(wk_sb[:], wk)
 
         cos_col = held.tile([P, 1], F32, name="cos_col")
         sin_col = held.tile([P, 1], F32, name="sin_col")
@@ -56,7 +56,7 @@ def tile_llamamodel_kernel(tc, table, gain, wk, cosv, sinv, offs, out):
 
         wk_split = held.tile([D, 2, PAIRS], BF16, name="wk_split")
         wk_pairs = wk_sb[:].rearrange("d (b q i two) -> d two b i q", b=GROUPS, q=HEADS_IN_GROUP, two=2)
-        for two in range(2):
+        for two in (1, 0):
             nc.gpsimd.tensor_copy(
                 wk_split[:, two, :].rearrange("d (b i q) -> d b i q", b=GROUPS, q=HEADS_IN_GROUP), wk_pairs[:, two]
             )

@@ -57,8 +57,13 @@ def tile_llamamodel_kernel(tc, table, gain, wk, cosv, sinv, offs, out):
         wk_split = held.tile([D, 2, PAIRS], BF16, name="wk_split")
         wk_pairs = wk_sb[:].rearrange("d (b q i two) -> d two b i q", b=GROUPS, q=HEADS_IN_GROUP, two=2)
         for two in (1, 0):
-            nc.gpsimd.tensor_copy(
-                wk_split[:, two, :].rearrange("d (b i q) -> d b i q", b=GROUPS, q=HEADS_IN_GROUP), wk_pairs[:, two]
+            nc.gpsimd.tensor_scalar(
+                wk_split[:, two, :].rearrange("d (b i q) -> d b i q", b=GROUPS, q=HEADS_IN_GROUP),
+                wk_pairs[:, two],
+                1.0,
+                0.0,
+                MULT,
+                ADD,
             )
 
         sumsq = held.tile([P, BLOCKS], F32, name="sumsq")

import concourse.mybir as mybir
from concourse.masks import make_identity

P = 128
V, D, M, N = 1024, 128, 512, 512
HALF = 32
EPS = 1e-5
FLOPS = 2 * D * M * N

BF16, F32, U16 = mybir.dt.bfloat16, mybir.dt.float32, mybir.dt.uint16
MULT, ADD, SUBTRACT = mybir.AluOpType.mult, mybir.AluOpType.add, mybir.AluOpType.subtract
ACT = mybir.ActivationFunctionType

BLOCKS = V // P
PAIRS_OF_BLOCKS = BLOCKS // 2
PAIRS = M // 2
GROUPS = PAIRS // P
HEADS_IN_GROUP = P // HALF


def tile_llamamodel_kernel(tc, table, gain, wk, cosv, sinv, offs, out):
    nc = tc.nc
    with (
        tc.tile_pool(name="held", bufs=1) as held,
        tc.tile_pool(name="work", bufs=2) as work,
        tc.psum_pool(name="flip", bufs=4) as flip,
        tc.psum_pool(name="keys", bufs=2) as keys,
    ):
        identity = held.tile([P, P], F32, name="identity")
        make_identity(nc, identity[:])

        rows = held.tile([P, BLOCKS, D], BF16, name="rows")
        table_runs = table.rearrange("(g p side) d -> p g (side d)", p=P, side=2)
        rows_runs = rows[:].rearrange("p (g side) d -> p g (side d)", side=2)
        for g in range(PAIRS_OF_BLOCKS):
            nc.sync.dma_start(rows_runs[:, g : g + 1, :], table_runs[:, g : g + 1, :])

        wk_sb = held.tile([D, M], BF16, name="wk_sb")
        nc.sync.dma_start(wk_sb[:], wk)

        offsets = held.tile([P, N // 16], U16, name="offsets")
        nc.sync.dma_start(offsets[:], offs)

        gain_col = held.tile([D, 1], F32, name="gain_col")
        nc.sync.dma_start(gain_col[:], gain)

        cos_col = held.tile([P, 1], F32, name="cos_col")
        sin_col = held.tile([P, 1], F32, name="sin_col")
        nc.sync.dma_start(cos_col[:], cosv.unsqueeze(1).broadcast_to([HALF, HEADS_IN_GROUP, 1]))
        nc.sync.dma_start(sin_col[:], sinv.unsqueeze(1).broadcast_to([HALF, HEADS_IN_GROUP, 1]))

        one = held.tile([P, 1], F32, name="one")
        nc.vector.memset(one[:], 1.0)
        unused = held.tile([P, 1], F32, name="unused")
        nc.scalar.activation(unused[:], one[:], ACT.Abs_reciprocal_sqrt)

        wk_split = held.tile([D, 2, PAIRS], BF16, name="wk_split")
        wk_pairs = wk_sb[:].rearrange("d (b q i two) -> d two b i q", b=GROUPS, q=HEADS_IN_GROUP, two=2)
        for two in (1, 0):
            nc.gpsimd.tensor_scalar(
                wk_split[:, two, :].rearrange("d (b i q) -> d b i q", b=GROUPS, q=HEADS_IN_GROUP),
                wk_pairs[:, two],
                1.0,
                0.0,
                MULT,
                ADD,
            )

        sumsq = held.tile([P, BLOCKS], F32, name="sumsq")
        rstd = held.tile([P, BLOCKS], F32, name="rstd")
        unit = held.tile([P, BLOCKS, D], F32, name="unit")
        window = held.tile([D, V], BF16, name="window")
        flipped_pairs = []

        def normalise_and_flip(g):
            k_s, k_v = 2 * g, 2 * g + 1
            sq_s = work.tile([P, D], F32, name="sq_s")
            nc.scalar.activation(sq_s[:], rows[:, k_s, :], ACT.Square, accum_out=sumsq[:, k_s : k_s + 1])
            sq_v = work.tile([P, D], F32, name="sq_v")
            nc.vector.scalar_tensor_tensor(
                sq_v[:], rows[:, k_v, :], 1.0, rows[:, k_v, :], MULT, MULT, accum_out=sumsq[:, k_v : k_v + 1]
            )
            nc.scalar.activation(
                rstd[:, k_s : k_v + 1], sumsq[:, k_s : k_v + 1], ACT.Abs_reciprocal_sqrt, bias=EPS, scale=1.0 / D
            )
            nc.scalar.activation(unit[:, k_s, :], rows[:, k_s, :], ACT.Copy, scale=rstd[:, k_s : k_s + 1])
            nc.vector.tensor_scalar(unit[:, k_v, :], rows[:, k_v, :], rstd[:, k_v : k_v + 1], None, MULT)
            flipped = flip.tile([D, 2 * P], F32, name="flipped")
            for side in range(2):
                nc.tensor.transpose(flipped[:, side * P : (side + 1) * P], unit[:, 2 * g + side, :], identity[:])
            flipped_pairs.append(flipped)

        def copy_out(g):
            xn = window[:, 2 * g * P : (2 * g + 2) * P].rearrange("d (p side) -> d p side", side=2)
            in_turn = flipped_pairs[g][:].rearrange("d (side p) -> d p side", side=2)
            if g % 2 == 0:
                nc.scalar.activation(xn, in_turn, ACT.Copy, scale=gain_col[:, 0:1])
            else:
                nc.vector.tensor_scalar(xn, in_turn, gain_col[:, 0:1], None, MULT)

        for g in range(PAIRS_OF_BLOCKS + 1):
            if g < PAIRS_OF_BLOCKS:
                normalise_and_flip(g)
            if g >= 1:
                copy_out(g - 1)

        out_rows = out.rearrange("(b q half i) j -> b half i q j", b=GROUPS, q=HEADS_IN_GROUP, half=2, i=HALF)
        for b in range(GROUPS):
            k_odd = keys.tile([P, N], F32, name="k_odd")
            nc.tensor.matmul(
                k_odd[:], wk_split[:, 1, b * P : (b + 1) * P], window[:].indirect(offsets[:]), start=True, stop=True
            )
            k_even = keys.tile([P, N], F32, name="k_even")
            nc.tensor.matmul(
                k_even[:], wk_split[:, 0, b * P : (b + 1) * P], window[:].indirect(offsets[:]), start=True, stop=True
            )
            odd_sin = work.tile([P, N], F32, name="odd_sin")
            nc.scalar.activation(odd_sin[:], k_odd[:], ACT.Copy, scale=sin_col[:, 0:1])
            odd_cos = work.tile([P, N], F32, name="odd_cos")
            nc.scalar.activation(odd_cos[:], k_odd[:], ACT.Copy, scale=cos_col[:, 0:1])
            first = work.tile([P, N], F32, name="first")
            nc.vector.scalar_tensor_tensor(first[:], k_even[:], cos_col[:, 0:1], odd_sin[:], MULT, SUBTRACT)
            second = work.tile([P, N], F32, name="second")
            nc.vector.scalar_tensor_tensor(second[:], k_even[:], sin_col[:, 0:1], odd_cos[:], MULT, ADD)
            for half, rotated in enumerate((first, second)):
                nc.sync.dma_start(out_rows[b, half], rotated[:])
